import numpy as np
import ml_dtypes


def mxq(x, axis, fmt="e4m3"):
    dtype, down = {"e4m3": (ml_dtypes.float8_e4m3fn, 7), "e5m2": (ml_dtypes.float8_e5m2, 14)}[fmt]
    v = np.moveaxis(np.asarray(x, np.float32).astype(ml_dtypes.bfloat16).astype(np.float64), axis, -1)
    blocks = v.reshape(v.shape[:-1] + (-1, 32))
    amax = np.abs(blocks).max(-1, keepdims=True)
    byte = np.maximum(np.where(amax > 0, np.frexp(amax)[1] - 1 + 127, 0) - down, 1)
    scale = np.exp2(byte - 127.0)
    codes = (blocks / scale).astype(np.float32).astype(dtype).astype(np.float64)
    return np.moveaxis((codes * scale).reshape(v.shape), -1, axis)


WIDE = False


def mx_kscale(k):
    if not WIDE:
        return np.ones(k)
    levels = np.array([10, -10, 5, -5, 0])
    a = np.random.permutation(np.resize(levels, k // 512 * 4)).reshape(k // 512, 4)
    idx = np.arange(k)
    return np.exp2(a[idx // 512, idx % 128 // 32])


BF16 = ml_dtypes.bfloat16


def bf(x):
    return np.asarray(x, np.float32).astype(BF16)


def f64(x):
    return np.asarray(x).astype(np.float64)


B, N, DIM, H, DH = 2, 2048, 1024, 4, 96
D1 = DH // 3


def rotate_half(t):
    d = t.shape[-1]
    t1, t2 = t[..., : (d + 1) // 2], t[..., (d + 1) // 2:]
    return np.concatenate((-t2, t1), axis=-1)


def apply_rope(t, freqs):
    return t * np.cos(freqs) + rotate_half(t) * np.sin(freqs)


def rope3(t, fs):
    return np.concatenate([apply_rope(ts, f) for ts, f in zip(np.split(t, (D1, 2 * D1), axis=-1), fs)], axis=-1)


def setup_inputs():
    s = mx_kscale(DIM)
    return {"x": bf(np.random.standard_normal((B, N, DIM)) * s),
            "f1": bf(np.random.uniform(0.0, 1.0, (N, D1))),
            "f2": bf(np.random.uniform(0.0, 1.0, (N, D1))),
            "f3": bf(np.random.uniform(0.0, 1.0, (N, D1))),
            "Wqkv": bf(np.random.standard_normal((DIM, 3 * H * DH)) / np.sqrt(DIM) / s[:, None])}


def reference(x, f1, f2, f3, Wqkv):
    qkv = mxq(f64(x), 2, "e4m3") @ mxq(f64(Wqkv), 0, "e4m3")
    q, k, v = np.split(qkv, 3, axis=-1)
    to_heads = lambda t: t.reshape(B, N, H, DH).transpose(0, 2, 1, 3)
    q, k, v = to_heads(q), to_heads(k), to_heads(v)
    fs = (f64(f1), f64(f2), f64(f3))
    return rope3(q, fs), rope3(k, fs), v

@@ -1,0 +1,213 @@
+import math
+from contextlib import ExitStack
+
+import concourse.mybir as mybir
+from concourse.masks import make_identity
+
+F32 = mybir.dt.float32
+BF16 = mybir.dt.bfloat16
+U32 = mybir.dt.uint32
+U8 = mybir.dt.uint8
+FP8X4 = mybir.dt.float8_e4m3fn_x4
+MULT = mybir.AluOpType.mult
+ADD = mybir.AluOpType.add
+SIN = mybir.ActivationFunctionType.Sin
+
+BATCH = 2
+TOKENS = 2048
+DIM = 1024
+HEADS = 4
+HEAD_DIM = 96
+AXES = 3
+AXIS_DIM = HEAD_DIM // AXES
+HALF = AXIS_DIM // 2
+
+P = 128
+PACK = 4
+K_PASS = P * PACK
+PASSES = DIM // K_PASS
+BLOCK = HEADS * HEAD_DIM
+COLS = 3 * BLOCK
+PARTS = ((0, 256), (256, 128))
+BANK = 512
+
+TILES = TOKENS // P
+PAIR = 2
+PAIRS = BATCH * TILES // PAIR
+GROUP = 4
+
+FLOPS = 2 * BATCH * TOKENS * DIM * COLS
+
+
+def tile_attention_pa_t_kernel(tc, x, f1, f2, f3, Wqkv, out_0, out_1, out_2):
+    nc = tc.nc
+    outs = (out_0, out_1, out_2)
+
+    with ExitStack() as ctx:
+        const = ctx.enter_context(tc.tile_pool(name="const", bufs=1))
+        x_pool = ctx.enter_context(tc.tile_pool(name="x", bufs=PAIRS))
+        work = ctx.enter_context(tc.tile_pool(name="work", bufs=3))
+        psum = ctx.enter_context(tc.psum_pool(name="psum", bufs=2))
+
+        def load_x_pair(i):
+            b, t = divmod(i * PAIR, TILES)
+            x_pair = x_pool.tile([P, PAIR, DIM], BF16)
+            by_partition = x[b].rearrange("(p t) k -> p t k", t=TILES)
+            nc.sync.dma_start(out=x_pair[:], in_=by_partition[:, t : t + PAIR, :])
+            return x_pair
+
+        angles = const.tile([P, AXES, TILES, AXIS_DIM], BF16)
+        for axis, f in enumerate((f1, f2, f3)):
+            nc.sync.dma_start(out=angles[:, axis], in_=f.rearrange("(p t) j -> p t j", t=TILES))
+
+        x_pairs = [load_x_pair(0)]
+
+        w_rows = const.tile([P, PASSES * PACK, COLS], BF16)
+        for gu in range(PASSES * 2):
+            nc.sync.dma_start(
+                out=w_rows[:, 2 * gu : 2 * gu + 2, :],
+                in_=Wqkv[2 * P * gu : 2 * P * (gu + 1), :].rearrange("(p e) c -> p e c", e=2),
+            )
+
+        for i in range(1, PAIRS):
+            x_pairs.append(load_x_pair(i))
+
+        ident = const.tile([P, P], F32)
+        make_identity(nc, ident[:])
+
+        def transpose_pair(i):
+            grouped = work.tile([P, PAIR, PASSES, P, PACK], BF16, align_bytes=64)
+            for a in range(PAIR):
+                words = x_pairs[i][:, a, :].bitcast(F32)
+                xt = psum.tile([P, PASSES * 2, P], F32)
+                for gu in range(PASSES * 2):
+                    nc.tensor.transpose(xt[:, gu, :], words[:, P * gu : P * (gu + 1)], ident[:])
+                nc.scalar.copy(
+                    out=grouped[:, a].bitcast(F32),
+                    in_=xt[:].rearrange("p (g u) r -> p g r u", u=2),
+                )
+            return grouped
+
+        def quantise_pair(grouped):
+            x_codes = work.tile([P, PAIR, PASSES, P], U32, align_bytes=64)
+            x_scales = work.tile([P, PAIR, PASSES, P], U8, align_bytes=64)
+            nc.vector.quantize_mx(
+                out=x_codes[:].rearrange("p a g r -> p (a g r)").bitcast(FP8X4),
+                scales=x_scales[:].rearrange("p a g r -> p (a g r)"),
+                in_=grouped[:].rearrange("p a g r t -> p (a g r t)"),
+            )
+            return x_codes, x_scales
+
+        ready = quantise_pair(transpose_pair(0))
+
+        factors = const.tile([P, TILES, 2, HEAD_DIM], F32)
+        by_tile = angles[:].rearrange("p a t j -> p t a j")
+        own = factors[:, :, 0, :].rearrange("p t (a j) -> p t a j", a=AXES)
+        partner = factors[:, :, 1, :].rearrange("p t (a j) -> p t a j", a=AXES)
+        nc.scalar.activation(out=own, in_=by_tile, func=SIN, bias=math.pi / 2, scale=-1.0)
+        nc.scalar.activation(out=partner[:, :, :, :HALF], in_=by_tile[:, :, :, HALF:], func=SIN)
+        nc.scalar.activation(
+            out=partner[:, :, :, HALF:], in_=by_tile[:, :, :, :HALF], func=SIN, scale=-1.0
+        )
+
+        w_grouped = const.tile([P, PASSES, COLS, PACK], BF16, align_bytes=64)
+        w_codes = const.tile([P, PASSES, COLS], U32, align_bytes=64)
+        w_scales = const.tile([P, PASSES, COLS], U8, align_bytes=64)
+
+        def regroup_views(g, s, part):
+            c0, width = part
+            cols = slice(BLOCK * s + c0, BLOCK * s + c0 + width)
+            rows = w_rows[:, PACK * g : PACK * (g + 1), cols]
+            return (
+                w_grouped[:, g, cols, :].rearrange("p (c i) t -> p c t i", i=4),
+                rows.rearrange("p t (c i) -> p c t i", i=4),
+            )
+
+        def regroup_w(g, s):
+            wide_out, wide_in = regroup_views(g, s, PARTS[0])
+            nc.vector.tensor_copy(out=wide_out, in_=wide_in)
+            narrow_out, narrow_in = regroup_views(g, s, PARTS[1])
+            nc.scalar.copy(out=narrow_out, in_=narrow_in)
+
+        def quantise_w(g, s):
+            for c0, width in PARTS:
+                cols = slice(BLOCK * s + c0, BLOCK * s + c0 + width)
+                nc.vector.quantize_mx(
+                    out=w_codes[:, g, cols].bitcast(FP8X4),
+                    scales=w_scales[:, g, cols],
+                    in_=w_grouped[:, g, cols, :].rearrange("p c t -> p (c t)"),
+                )
+
+        pieces = [(g, s) for g in range(PASSES) for s in range(3)]
+        for n, (g, s) in enumerate(pieces):
+            regroup_w(g, s)
+            if n > 0:
+                quantise_w(*pieces[n - 1])
+        quantise_w(*pieces[-1])
+
+        def project(x_codes, x_scales, a):
+            ps_q = psum.tile([P, BANK], F32)
+            ps_k = psum.tile([P, BANK], F32)
+            ps_v = psum.tile([P, BANK], F32)
+            for c0, width in PARTS:
+                for s, bank in enumerate((ps_q, ps_k, ps_v)):
+                    cols = slice(BLOCK * s + c0, BLOCK * s + c0 + width)
+                    for g in range(PASSES):
+                        nc.tensor.matmul_mx(
+                            out=bank[:, c0 : c0 + width],
+                            lhsT=x_codes[:, a, g, :].bitcast(FP8X4),
+                            lhsT_scale=x_scales[:, a, g, :],
+                            rhs=w_codes[:, g, cols].bitcast(FP8X4),
+                            rhs_scale=w_scales[:, g, cols],
+                            start=(g == 0),
+                            stop=(g == PASSES - 1),
+                        )
+            return ps_q, ps_k, ps_v
+
+        def rope_and_collect(banks, t, staged, slot):
+            ps_q, ps_k, ps_v = banks
+            products = work.tile([P, 2, 2, BLOCK], F32)
+            shape = [P, 2, HEADS, HEAD_DIM]
+            for s, bank in enumerate((ps_q, ps_k)):
+                by_head = bank[:, :BLOCK].rearrange("p (h d) -> p h d", h=HEADS)
+                nc.vector.tensor_tensor(
+                    out=products[:, :, s, :].rearrange("p c (h d) -> p c h d", h=HEADS),
+                    in0=by_head.unsqueeze(1).to_broadcast(shape),
+                    in1=factors[:, t].unsqueeze(2).to_broadcast(shape),
+                    op=MULT,
+                )
+            split = "p s (h a f j) -> p (s h) a f j"
+            own_part = products[:, 0].rearrange(split, h=HEADS, a=AXES, f=2)
+            partner_part = products[:, 1].rearrange(split, h=HEADS, a=AXES, f=2)
+            rotated = staged[:, 0:2, :, slot, :].rearrange(
+                "p s h (a f j) -> p (s h) a f j", a=AXES, f=2
+            )
+            for f in range(2):
+                nc.gpsimd.tensor_tensor(
+                    out=rotated[:, :, :, f, :],
+                    in0=own_part[:, :, :, f, :],
+                    in1=partner_part[:, :, :, 1 - f, :],
+                    op=ADD,
+                )
+            nc.scalar.copy(
+                out=staged[:, 2, :, slot, :],
+                in_=ps_v[:, :BLOCK].rearrange("p (h d) -> p h d", h=HEADS),
+            )
+
+        staged = None
+        for i in range(PAIRS):
+            x_codes, x_scales = ready
+            if i + 1 < PAIRS:
+                ready = quantise_pair(transpose_pair(i + 1))
+            for a in range(PAIR):
+                b, t = divmod(i * PAIR + a, TILES)
+                slot = t % GROUP
+                if slot == 0:
+                    staged = work.tile([P, 3, HEADS, GROUP, HEAD_DIM], F32)
+                rope_and_collect(project(x_codes, x_scales, a), t, staged, slot)
+                if slot == GROUP - 1:
+                    for s, out in enumerate(outs):
+                        by_partition = out[b].rearrange("h (p t) d -> p h t d", t=TILES)
+                        nc.sync.dma_start(
+                            out=by_partition[:, :, t - slot : t + 1, :], in_=staged[:, s]
+                        )

@@ -47,6 +47,7 @@ def tile_attention_pa_t_kernel(tc, x, f1, f2, f3, Wqkv, out_0, out_1, out_2):
         const = ctx.enter_context(tc.tile_pool(name="const", bufs=1))
         x_pool = ctx.enter_context(tc.tile_pool(name="x", bufs=PAIRS))
         work = ctx.enter_context(tc.tile_pool(name="work", bufs=3))
+        product_pool = ctx.enter_context(tc.tile_pool(name="products", bufs=2))
         psum = ctx.enter_context(tc.psum_pool(name="psum", bufs=2))
 
         def load_x_pair(i):
@@ -62,15 +63,32 @@ def tile_attention_pa_t_kernel(tc, x, f1, f2, f3, Wqkv, out_0, out_1, out_2):
 
         x_pairs = [load_x_pair(0)]
 
-        w_rows = const.tile([P, PASSES * PACK, COLS], BF16)
-        for gu in range(PASSES * 2):
-            nc.sync.dma_start(
-                out=w_rows[:, 2 * gu : 2 * gu + 2, :],
-                in_=Wqkv[2 * P * gu : 2 * P * (gu + 1), :].rearrange("(p e) c -> p e c", e=2),
-            )
+        w_rows = const.tile([P, 3, PASSES * PACK, BLOCK], BF16)
+        for s in range(3):
+            for gu in range(PASSES * 2):
+                rows = Wqkv[2 * P * gu : 2 * P * (gu + 1), BLOCK * s : BLOCK * (s + 1)]
+                nc.sync.dma_start(
+                    out=w_rows[:, s, 2 * gu : 2 * gu + 2, :],
+                    in_=rows.rearrange("(p e) c -> p e c", e=2),
+                )
 
         for i in range(1, PAIRS):
             x_pairs.append(load_x_pair(i))
+
+        factors = const.tile([P, TILES, 2, HEAD_DIM], F32)
+
+        def make_factors(group):
+            tiles = slice(GROUP * group, GROUP * (group + 1))
+            angle = angles[:, :, tiles, :].rearrange("p a t j -> p t a j")
+            own = factors[:, tiles, 0, :].rearrange("p t (a j) -> p t a j", a=AXES)
+            partner = factors[:, tiles, 1, :].rearrange("p t (a j) -> p t a j", a=AXES)
+            nc.scalar.activation(out=own, in_=angle, func=SIN, bias=math.pi / 2, scale=-1.0)
+            nc.scalar.activation(out=partner[:, :, :, :HALF], in_=angle[:, :, :, HALF:], func=SIN)
+            nc.scalar.activation(
+                out=partner[:, :, :, HALF:], in_=angle[:, :, :, :HALF], func=SIN, scale=-1.0
+            )
+
+        make_factors(0)
 
         ident = const.tile([P, P], F32)
         make_identity(nc, ident[:])
@@ -100,47 +118,35 @@ def tile_attention_pa_t_kernel(tc, x, f1, f2, f3, Wqkv, out_0, out_1, out_2):
 
         ready = quantise_pair(transpose_pair(0))
 
-        factors = const.tile([P, TILES, 2, HEAD_DIM], F32)
-        by_tile = angles[:].rearrange("p a t j -> p t a j")
-        own = factors[:, :, 0, :].rearrange("p t (a j) -> p t a j", a=AXES)
-        partner = factors[:, :, 1, :].rearrange("p t (a j) -> p t a j", a=AXES)
-        nc.scalar.activation(out=own, in_=by_tile, func=SIN, bias=math.pi / 2, scale=-1.0)
-        nc.scalar.activation(out=partner[:, :, :, :HALF], in_=by_tile[:, :, :, HALF:], func=SIN)
-        nc.scalar.activation(
-            out=partner[:, :, :, HALF:], in_=by_tile[:, :, :, :HALF], func=SIN, scale=-1.0
-        )
+        w_grouped = const.tile([P, 3, PASSES, BLOCK, PACK], BF16, align_bytes=64)
+        w_codes = const.tile([P, 3, PASSES, BLOCK], U32, align_bytes=64)
+        w_scales = const.tile([P, 3, PASSES, BLOCK], U8, align_bytes=64)
 
-        w_grouped = const.tile([P, PASSES, COLS, PACK], BF16, align_bytes=64)
-        w_codes = const.tile([P, PASSES, COLS], U32, align_bytes=64)
-        w_scales = const.tile([P, PASSES, COLS], U8, align_bytes=64)
-
-        def regroup_views(g, s, part):
+        def regroup_views(s, g, part):
             c0, width = part
-            cols = slice(BLOCK * s + c0, BLOCK * s + c0 + width)
-            rows = w_rows[:, PACK * g : PACK * (g + 1), cols]
+            rows = w_rows[:, s, PACK * g : PACK * (g + 1), c0 : c0 + width]
             return (
-                w_grouped[:, g, cols, :].rearrange("p (c i) t -> p c t i", i=4),
+                w_grouped[:, s, g, c0 : c0 + width, :].rearrange("p (c i) t -> p c t i", i=4),
                 rows.rearrange("p t (c i) -> p c t i", i=4),
             )
 
-        def regroup_w(g, s):
-            wide_out, wide_in = regroup_views(g, s, PARTS[0])
+        def regroup_w(s, g):
+            wide_out, wide_in = regroup_views(s, g, PARTS[0])
             nc.vector.tensor_copy(out=wide_out, in_=wide_in)
-            narrow_out, narrow_in = regroup_views(g, s, PARTS[1])
+            narrow_out, narrow_in = regroup_views(s, g, PARTS[1])
             nc.scalar.copy(out=narrow_out, in_=narrow_in)
 
-        def quantise_w(g, s):
+        def quantise_w(s, g):
             for c0, width in PARTS:
-                cols = slice(BLOCK * s + c0, BLOCK * s + c0 + width)
                 nc.vector.quantize_mx(
-                    out=w_codes[:, g, cols].bitcast(FP8X4),
-                    scales=w_scales[:, g, cols],
-                    in_=w_grouped[:, g, cols, :].rearrange("p c t -> p (c t)"),
+                    out=w_codes[:, s, g, c0 : c0 + width].bitcast(FP8X4),
+                    scales=w_scales[:, s, g, c0 : c0 + width],
+                    in_=w_grouped[:, s, g, c0 : c0 + width, :].rearrange("p c t -> p (c t)"),
                 )
 
-        pieces = [(g, s) for g in range(PASSES) for s in range(3)]
-        for n, (g, s) in enumerate(pieces):
-            regroup_w(g, s)
+        pieces = [(s, g) for s in range(3) for g in range(PASSES)]
+        for n, (s, g) in enumerate(pieces):
+            regroup_w(s, g)
             if n > 0:
                 quantise_w(*pieces[n - 1])
         quantise_w(*pieces[-1])
@@ -149,65 +155,81 @@ def tile_attention_pa_t_kernel(tc, x, f1, f2, f3, Wqkv, out_0, out_1, out_2):
             ps_q = psum.tile([P, BANK], F32)
             ps_k = psum.tile([P, BANK], F32)
             ps_v = psum.tile([P, BANK], F32)
-            for c0, width in PARTS:
-                for s, bank in enumerate((ps_q, ps_k, ps_v)):
-                    cols = slice(BLOCK * s + c0, BLOCK * s + c0 + width)
+            for s, bank in enumerate((ps_q, ps_k, ps_v)):
+                for c0, width in PARTS:
                     for g in range(PASSES):
                         nc.tensor.matmul_mx(
                             out=bank[:, c0 : c0 + width],
                             lhsT=x_codes[:, a, g, :].bitcast(FP8X4),
                             lhsT_scale=x_scales[:, a, g, :],
-                            rhs=w_codes[:, g, cols].bitcast(FP8X4),
-                            rhs_scale=w_scales[:, g, cols],
+                            rhs=w_codes[:, s, g, c0 : c0 + width].bitcast(FP8X4),
+                            rhs_scale=w_scales[:, s, g, c0 : c0 + width],
                             start=(g == 0),
                             stop=(g == PASSES - 1),
                         )
             return ps_q, ps_k, ps_v
 
-        def rope_and_collect(banks, t, staged, slot):
-            ps_q, ps_k, ps_v = banks
-            products = work.tile([P, 2, 2, BLOCK], F32)
+        def multiply(ps_q, ps_k, t, products, a):
             shape = [P, 2, HEADS, HEAD_DIM]
             for s, bank in enumerate((ps_q, ps_k)):
                 by_head = bank[:, :BLOCK].rearrange("p (h d) -> p h d", h=HEADS)
                 nc.vector.tensor_tensor(
-                    out=products[:, :, s, :].rearrange("p c (h d) -> p c h d", h=HEADS),
+                    out=products[:, :, s, :, a, :],
                     in0=by_head.unsqueeze(1).to_broadcast(shape),
                     in1=factors[:, t].unsqueeze(2).to_broadcast(shape),
                     op=MULT,
                 )
-            split = "p s (h a f j) -> p (s h) a f j"
-            own_part = products[:, 0].rearrange(split, h=HEADS, a=AXES, f=2)
-            partner_part = products[:, 1].rearrange(split, h=HEADS, a=AXES, f=2)
-            rotated = staged[:, 0:2, :, slot, :].rearrange(
-                "p s h (a f j) -> p (s h) a f j", a=AXES, f=2
-            )
+
+        def add_partners(products, a0, count, staged, slot0):
+            split = "p s h a (x f j) -> p (s h) (a x) f j"
+            tiles = slice(a0, a0 + count)
+            slots = slice(slot0 + a0, slot0 + a0 + count)
+            own = products[:, 0, :, :, tiles, :].rearrange(split, x=AXES, f=2)
+            partner = products[:, 1, :, :, tiles, :].rearrange(split, x=AXES, f=2)
+            rotated = staged[:, 0:2, :, slots, :].rearrange(split, x=AXES, f=2)
             for f in range(2):
                 nc.gpsimd.tensor_tensor(
                     out=rotated[:, :, :, f, :],
-                    in0=own_part[:, :, :, f, :],
-                    in1=partner_part[:, :, :, 1 - f, :],
+                    in0=own[:, :, :, f, :],
+                    in1=partner[:, :, :, 1 - f, :],
                     op=ADD,
                 )
-            nc.scalar.copy(
-                out=staged[:, 2, :, slot, :],
-                in_=ps_v[:, :BLOCK].rearrange("p (h d) -> p h d", h=HEADS),
-            )
+
+        def store(b, t0, count, staged, slot0):
+            for s, out in enumerate(outs):
+                by_partition = out[b].rearrange("h (p t) d -> p h t d", t=TILES)
+                nc.sync.dma_start(
+                    out=by_partition[:, :, t0 : t0 + count, :],
+                    in_=staged[:, s, :, slot0 : slot0 + count, :],
+                )
 
         staged = None
         for i in range(PAIRS):
             x_codes, x_scales = ready
             if i + 1 < PAIRS:
                 ready = quantise_pair(transpose_pair(i + 1))
+            b, t0 = divmod(i * PAIR, TILES)
+            slot0 = t0 % GROUP
+            if slot0 == 0:
+                staged = work.tile([P, 3, HEADS, GROUP, HEAD_DIM], F32)
+                next_group = t0 // GROUP + 1
+                if b == 0 and next_group < TILES // GROUP:
+                    make_factors(next_group)
+            products = product_pool.tile([P, 2, 2, HEADS, PAIR, HEAD_DIM], F32)
+            last_pair = i == PAIRS - 1
+            last_group = i * PAIR >= BATCH * TILES - GROUP
             for a in range(PAIR):
-                b, t = divmod(i * PAIR + a, TILES)
-                slot = t % GROUP
-                if slot == 0:
-                    staged = work.tile([P, 3, HEADS, GROUP, HEAD_DIM], F32)
-                rope_and_collect(project(x_codes, x_scales, a), t, staged, slot)
-                if slot == GROUP - 1:
-                    for s, out in enumerate(outs):
-                        by_partition = out[b].rearrange("h (p t) d -> p h t d", t=TILES)
-                        nc.sync.dma_start(
-                            out=by_partition[:, :, t - slot : t + 1, :], in_=staged[:, s]
-                        )
+                ps_q, ps_k, ps_v = project(x_codes, x_scales, a)
+                multiply(ps_q, ps_k, t0 + a, products, a)
+                nc.scalar.copy(
+                    out=staged[:, 2, :, slot0 + a, :],
+                    in_=ps_v[:, :BLOCK].rearrange("p (h d) -> p h d", h=HEADS),
+                )
+                if last_pair:
+                    add_partners(products, a, 1, staged, slot0)
+            if not last_pair:
+                add_partners(products, 0, PAIR, staged, slot0)
+            if last_group:
+                store(b, t0, PAIR, staged, slot0)
+            elif slot0 + PAIR == GROUP:
+                store(b, t0 + PAIR - GROUP, GROUP, staged, 0)

@@ -47,8 +47,8 @@ def tile_attention_pa_t_kernel(tc, x, f1, f2, f3, Wqkv, out_0, out_1, out_2):
         const = ctx.enter_context(tc.tile_pool(name="const", bufs=1))
         x_pool = ctx.enter_context(tc.tile_pool(name="x", bufs=PAIRS))
         work = ctx.enter_context(tc.tile_pool(name="work", bufs=3))
-        product_pool = ctx.enter_context(tc.tile_pool(name="products", bufs=2))
         psum = ctx.enter_context(tc.psum_pool(name="psum", bufs=2))
+        ctx.enter_context(tc.manual_schedule())
 
         def load_x_pair(i):
             b, t = divmod(i * PAIR, TILES)
@@ -63,14 +63,12 @@ def tile_attention_pa_t_kernel(tc, x, f1, f2, f3, Wqkv, out_0, out_1, out_2):
 
         x_pairs = [load_x_pair(0)]
 
-        w_rows = const.tile([P, 3, PASSES * PACK, BLOCK], BF16)
-        for s in range(3):
-            for gu in range(PASSES * 2):
-                rows = Wqkv[2 * P * gu : 2 * P * (gu + 1), BLOCK * s : BLOCK * (s + 1)]
-                nc.sync.dma_start(
-                    out=w_rows[:, s, 2 * gu : 2 * gu + 2, :],
-                    in_=rows.rearrange("(p e) c -> p e c", e=2),
-                )
+        w_rows = const.tile([P, PASSES * PACK, COLS], BF16)
+        for gu in range(PASSES * 2):
+            nc.sync.dma_start(
+                out=w_rows[:, 2 * gu : 2 * gu + 2, :],
+                in_=Wqkv[2 * P * gu : 2 * P * (gu + 1), :].rearrange("(p e) c -> p e c", e=2),
+            )
 
         for i in range(1, PAIRS):
             x_pairs.append(load_x_pair(i))
@@ -116,40 +114,43 @@ def tile_attention_pa_t_kernel(tc, x, f1, f2, f3, Wqkv, out_0, out_1, out_2):
             )
             return x_codes, x_scales
 
-        ready = quantise_pair(transpose_pair(0))
+        first_grouped = transpose_pair(0)
 
-        w_grouped = const.tile([P, 3, PASSES, BLOCK, PACK], BF16, align_bytes=64)
-        w_codes = const.tile([P, 3, PASSES, BLOCK], U32, align_bytes=64)
-        w_scales = const.tile([P, 3, PASSES, BLOCK], U8, align_bytes=64)
+        w_grouped = const.tile([P, PASSES, COLS, PACK], BF16, align_bytes=64)
+        w_codes = const.tile([P, PASSES, COLS], U32, align_bytes=64)
+        w_scales = const.tile([P, PASSES, COLS], U8, align_bytes=64)
 
-        def regroup_views(s, g, part):
+        def regroup_views(g, s, part):
             c0, width = part
-            rows = w_rows[:, s, PACK * g : PACK * (g + 1), c0 : c0 + width]
+            cols = slice(BLOCK * s + c0, BLOCK * s + c0 + width)
+            rows = w_rows[:, PACK * g : PACK * (g + 1), cols]
             return (
-                w_grouped[:, s, g, c0 : c0 + width, :].rearrange("p (c i) t -> p c t i", i=4),
+                w_grouped[:, g, cols, :].rearrange("p (c i) t -> p c t i", i=4),
                 rows.rearrange("p t (c i) -> p c t i", i=4),
             )
 
-        def regroup_w(s, g):
-            wide_out, wide_in = regroup_views(s, g, PARTS[0])
+        def regroup_w(g, s):
+            wide_out, wide_in = regroup_views(g, s, PARTS[0])
             nc.vector.tensor_copy(out=wide_out, in_=wide_in)
-            narrow_out, narrow_in = regroup_views(s, g, PARTS[1])
+            narrow_out, narrow_in = regroup_views(g, s, PARTS[1])
             nc.scalar.copy(out=narrow_out, in_=narrow_in)
 
-        def quantise_w(s, g):
+        def quantise_w(g, s):
             for c0, width in PARTS:
+                cols = slice(BLOCK * s + c0, BLOCK * s + c0 + width)
                 nc.vector.quantize_mx(
-                    out=w_codes[:, s, g, c0 : c0 + width].bitcast(FP8X4),
-                    scales=w_scales[:, s, g, c0 : c0 + width],
-                    in_=w_grouped[:, s, g, c0 : c0 + width, :].rearrange("p c t -> p (c t)"),
+                    out=w_codes[:, g, cols].bitcast(FP8X4),
+                    scales=w_scales[:, g, cols],
+                    in_=w_grouped[:, g, cols, :].rearrange("p c t -> p (c t)"),
                 )
 
-        pieces = [(s, g) for s in range(3) for g in range(PASSES)]
-        for n, (s, g) in enumerate(pieces):
-            regroup_w(s, g)
+        pieces = [(g, s) for g in range(PASSES) for s in range(3)]
+        for n, (g, s) in enumerate(pieces):
+            regroup_w(g, s)
             if n > 0:
                 quantise_w(*pieces[n - 1])
         quantise_w(*pieces[-1])
+        ready = quantise_pair(first_grouped)
 
         def project(x_codes, x_scales, a):
             ps_q = psum.tile([P, BANK], F32)
@@ -157,43 +158,48 @@ def tile_attention_pa_t_kernel(tc, x, f1, f2, f3, Wqkv, out_0, out_1, out_2):
             ps_v = psum.tile([P, BANK], F32)
             for s, bank in enumerate((ps_q, ps_k, ps_v)):
                 for c0, width in PARTS:
+                    cols = slice(BLOCK * s + c0, BLOCK * s + c0 + width)
                     for g in range(PASSES):
                         nc.tensor.matmul_mx(
                             out=bank[:, c0 : c0 + width],
                             lhsT=x_codes[:, a, g, :].bitcast(FP8X4),
                             lhsT_scale=x_scales[:, a, g, :],
-                            rhs=w_codes[:, s, g, c0 : c0 + width].bitcast(FP8X4),
-                            rhs_scale=w_scales[:, s, g, c0 : c0 + width],
+                            rhs=w_codes[:, g, cols].bitcast(FP8X4),
+                            rhs_scale=w_scales[:, g, cols],
                             start=(g == 0),
                             stop=(g == PASSES - 1),
                         )
             return ps_q, ps_k, ps_v
 
-        def multiply(ps_q, ps_k, t, products, a):
+        def rope_and_collect(banks, t, staged, slot):
+            ps_q, ps_k, ps_v = banks
+            products = work.tile([P, 2, 2, BLOCK], F32)
             shape = [P, 2, HEADS, HEAD_DIM]
             for s, bank in enumerate((ps_q, ps_k)):
                 by_head = bank[:, :BLOCK].rearrange("p (h d) -> p h d", h=HEADS)
                 nc.vector.tensor_tensor(
-                    out=products[:, :, s, :, a, :],
+                    out=products[:, :, s, :].rearrange("p c (h d) -> p c h d", h=HEADS),
                     in0=by_head.unsqueeze(1).to_broadcast(shape),
                     in1=factors[:, t].unsqueeze(2).to_broadcast(shape),
                     op=MULT,
                 )
-
-        def add_partners(products, a0, count, staged, slot0):
-            split = "p s h a (x f j) -> p (s h) (a x) f j"
-            tiles = slice(a0, a0 + count)
-            slots = slice(slot0 + a0, slot0 + a0 + count)
-            own = products[:, 0, :, :, tiles, :].rearrange(split, x=AXES, f=2)
-            partner = products[:, 1, :, :, tiles, :].rearrange(split, x=AXES, f=2)
-            rotated = staged[:, 0:2, :, slots, :].rearrange(split, x=AXES, f=2)
+            split = "p s (h a f j) -> p (s h) a f j"
+            own_part = products[:, 0].rearrange(split, h=HEADS, a=AXES, f=2)
+            partner_part = products[:, 1].rearrange(split, h=HEADS, a=AXES, f=2)
+            rotated = staged[:, 0:2, :, slot, :].rearrange(
+                "p s h (a f j) -> p (s h) a f j", a=AXES, f=2
+            )
             for f in range(2):
                 nc.gpsimd.tensor_tensor(
                     out=rotated[:, :, :, f, :],
-                    in0=own[:, :, :, f, :],
-                    in1=partner[:, :, :, 1 - f, :],
+                    in0=own_part[:, :, :, f, :],
+                    in1=partner_part[:, :, :, 1 - f, :],
                     op=ADD,
                 )
+            nc.scalar.copy(
+                out=staged[:, 2, :, slot, :],
+                in_=ps_v[:, :BLOCK].rearrange("p (h d) -> p h d", h=HEADS),
+            )
 
         def store(b, t0, count, staged, slot0):
             for s, out in enumerate(outs):
@@ -206,8 +212,6 @@ def tile_attention_pa_t_kernel(tc, x, f1, f2, f3, Wqkv, out_0, out_1, out_2):
         staged = None
         for i in range(PAIRS):
             x_codes, x_scales = ready
-            if i + 1 < PAIRS:
-                ready = quantise_pair(transpose_pair(i + 1))
             b, t0 = divmod(i * PAIR, TILES)
             slot0 = t0 % GROUP
             if slot0 == 0:
@@ -215,21 +219,12 @@ def tile_attention_pa_t_kernel(tc, x, f1, f2, f3, Wqkv, out_0, out_1, out_2):
                 next_group = t0 // GROUP + 1
                 if b == 0 and next_group < TILES // GROUP:
                     make_factors(next_group)
-            products = product_pool.tile([P, 2, 2, HEADS, PAIR, HEAD_DIM], F32)
-            last_pair = i == PAIRS - 1
-            last_group = i * PAIR >= BATCH * TILES - GROUP
-            for a in range(PAIR):
-                ps_q, ps_k, ps_v = project(x_codes, x_scales, a)
-                multiply(ps_q, ps_k, t0 + a, products, a)
-                nc.scalar.copy(
-                    out=staged[:, 2, :, slot0 + a, :],
-                    in_=ps_v[:, :BLOCK].rearrange("p (h d) -> p h d", h=HEADS),
-                )
-                if last_pair:
-                    add_partners(products, a, 1, staged, slot0)
-            if not last_pair:
-                add_partners(products, 0, PAIR, staged, slot0)
-            if last_group:
+            grouped = transpose_pair(i + 1) if i + 1 < PAIRS else None
+            rope_and_collect(project(x_codes, x_scales, 0), t0, staged, slot0)
+            if grouped is not None:
+                ready = quantise_pair(grouped)
+            rope_and_collect(project(x_codes, x_scales, 1), t0 + 1, staged, slot0 + 1)
+            if i * PAIR >= BATCH * TILES - GROUP:
                 store(b, t0, PAIR, staged, slot0)
             elif slot0 + PAIR == GROUP:
                 store(b, t0 + PAIR - GROUP, GROUP, staged, 0)

@@ -35,6 +35,7 @@ TILES = TOKENS // P
 PAIR = 2
 PAIRS = BATCH * TILES // PAIR
 GROUP = 4
+VECTOR_ADDS_EVERY = 8
 
 FLOPS = 2 * BATCH * TOKENS * DIM * COLS
 
@@ -57,18 +58,18 @@ def tile_attention_pa_t_kernel(tc, x, f1, f2, f3, Wqkv, out_0, out_1, out_2):
             nc.sync.dma_start(out=x_pair[:], in_=by_partition[:, t : t + PAIR, :])
             return x_pair
 
-        angles = const.tile([P, AXES, TILES, AXIS_DIM], BF16)
-        for axis, f in enumerate((f1, f2, f3)):
-            nc.sync.dma_start(out=angles[:, axis], in_=f.rearrange("(p t) j -> p t j", t=TILES))
-
-        x_pairs = [load_x_pair(0)]
-
         w_rows = const.tile([P, PASSES * PACK, COLS], BF16)
         for gu in range(PASSES * 2):
             nc.sync.dma_start(
                 out=w_rows[:, 2 * gu : 2 * gu + 2, :],
                 in_=Wqkv[2 * P * gu : 2 * P * (gu + 1), :].rearrange("(p e) c -> p e c", e=2),
             )
+
+        x_pairs = [load_x_pair(0)]
+
+        angles = const.tile([P, AXES, TILES, AXIS_DIM], BF16)
+        for axis, f in enumerate((f1, f2, f3)):
+            nc.sync.dma_start(out=angles[:, axis], in_=f.rearrange("(p t) j -> p t j", t=TILES))
 
         for i in range(1, PAIRS):
             x_pairs.append(load_x_pair(i))
@@ -86,7 +87,9 @@ def tile_attention_pa_t_kernel(tc, x, f1, f2, f3, Wqkv, out_0, out_1, out_2):
                 out=partner[:, :, :, HALF:], in_=angle[:, :, :, :HALF], func=SIN, scale=-1.0
             )
 
-        make_factors(0)
+        warm = const.tile([P, 1], F32)
+        nc.vector.memset(warm[:], 0.0)
+        nc.scalar.activation(out=warm[:], in_=warm[:], func=SIN)
 
         ident = const.tile([P, P], F32)
         make_identity(nc, ident[:])
@@ -114,7 +117,6 @@ def tile_attention_pa_t_kernel(tc, x, f1, f2, f3, Wqkv, out_0, out_1, out_2):
             )
             return x_codes, x_scales
 
-        first_grouped = transpose_pair(0)
 
         w_grouped = const.tile([P, PASSES, COLS, PACK], BF16, align_bytes=64)
         w_codes = const.tile([P, PASSES, COLS], U32, align_bytes=64)
@@ -150,7 +152,8 @@ def tile_attention_pa_t_kernel(tc, x, f1, f2, f3, Wqkv, out_0, out_1, out_2):
             if n > 0:
                 quantise_w(*pieces[n - 1])
         quantise_w(*pieces[-1])
-        ready = quantise_pair(first_grouped)
+        ready = quantise_pair(transpose_pair(0))
+        make_factors(0)
 
         def project(x_codes, x_scales, a):
             ps_q = psum.tile([P, BANK], F32)
@@ -189,8 +192,9 @@ def tile_attention_pa_t_kernel(tc, x, f1, f2, f3, Wqkv, out_0, out_1, out_2):
             rotated = staged[:, 0:2, :, slot, :].rearrange(
                 "p s h (a f j) -> p (s h) a f j", a=AXES, f=2
             )
+            adder = nc.vector if t % VECTOR_ADDS_EVERY == VECTOR_ADDS_EVERY - 1 else nc.gpsimd
             for f in range(2):
-                nc.gpsimd.tensor_tensor(
+                adder.tensor_tensor(
                     out=rotated[:, :, :, f, :],
                     in0=own_part[:, :, :, f, :],
                     in1=partner_part[:, :, :, 1 - f, :],

import math
from contextlib import ExitStack

import concourse.mybir as mybir
from concourse.masks import make_identity

F32 = mybir.dt.float32
BF16 = mybir.dt.bfloat16
U32 = mybir.dt.uint32
U8 = mybir.dt.uint8
FP8X4 = mybir.dt.float8_e4m3fn_x4
MULT = mybir.AluOpType.mult
ADD = mybir.AluOpType.add
SIN = mybir.ActivationFunctionType.Sin

BATCH = 2
TOKENS = 2048
DIM = 1024
HEADS = 4
HEAD_DIM = 96
AXES = 3
AXIS_DIM = HEAD_DIM // AXES
HALF = AXIS_DIM // 2

P = 128
PACK = 4
K_PASS = P * PACK
PASSES = DIM // K_PASS
BLOCK = HEADS * HEAD_DIM
COLS = 3 * BLOCK
PARTS = ((0, 256), (256, 128))
BANK = 512

TILES = TOKENS // P
PAIR = 2
PAIRS = BATCH * TILES // PAIR
GROUP = 4
VECTOR_ADDS_EVERY = 8

FLOPS = 2 * BATCH * TOKENS * DIM * COLS


def tile_attention_pa_t_kernel(tc, x, f1, f2, f3, Wqkv, out_0, out_1, out_2):
    nc = tc.nc
    outs = (out_0, out_1, out_2)

    with ExitStack() as ctx:
        const = ctx.enter_context(tc.tile_pool(name="const", bufs=1))
        x_pool = ctx.enter_context(tc.tile_pool(name="x", bufs=PAIRS))
        work = ctx.enter_context(tc.tile_pool(name="work", bufs=3))
        psum = ctx.enter_context(tc.psum_pool(name="psum", bufs=2))
        ctx.enter_context(tc.manual_schedule())

        def load_x_pair(i):
            b, t = divmod(i * PAIR, TILES)
            x_pair = x_pool.tile([P, PAIR, DIM], BF16)
            by_partition = x[b].rearrange("(p t) k -> p t k", t=TILES)
            nc.sync.dma_start(out=x_pair[:], in_=by_partition[:, t : t + PAIR, :])
            return x_pair

        w_rows = const.tile([P, PASSES * PACK, COLS], BF16)
        for gu in range(PASSES * 2):
            nc.sync.dma_start(
                out=w_rows[:, 2 * gu : 2 * gu + 2, :],
                in_=Wqkv[2 * P * gu : 2 * P * (gu + 1), :].rearrange("(p e) c -> p e c", e=2),
            )

        x_pairs = [load_x_pair(0)]

        angles = const.tile([P, AXES, TILES, AXIS_DIM], BF16)
        for axis, f in enumerate((f1, f2, f3)):
            nc.sync.dma_start(out=angles[:, axis], in_=f.rearrange("(p t) j -> p t j", t=TILES))

        for i in range(1, PAIRS):
            x_pairs.append(load_x_pair(i))

        factors = const.tile([P, TILES, 2, HEAD_DIM], F32)

        def make_factors(group):
            tiles = slice(GROUP * group, GROUP * (group + 1))
            angle = angles[:, :, tiles, :].rearrange("p a t j -> p t a j")
            own = factors[:, tiles, 0, :].rearrange("p t (a j) -> p t a j", a=AXES)
            partner = factors[:, tiles, 1, :].rearrange("p t (a j) -> p t a j", a=AXES)
            nc.scalar.activation(out=own, in_=angle, func=SIN, bias=math.pi / 2, scale=-1.0)
            nc.scalar.activation(out=partner[:, :, :, :HALF], in_=angle[:, :, :, HALF:], func=SIN)
            nc.scalar.activation(
                out=partner[:, :, :, HALF:], in_=angle[:, :, :, :HALF], func=SIN, scale=-1.0
            )

        warm = const.tile([P, 1], F32)
        nc.vector.memset(warm[:], 0.0)
        nc.scalar.activation(out=warm[:], in_=warm[:], func=SIN)

        ident = const.tile([P, P], F32)
        make_identity(nc, ident[:])

        def transpose_pair(i):
            grouped = work.tile([P, PAIR, PASSES, P, PACK], BF16, align_bytes=64)
            for a in range(PAIR):
                words = x_pairs[i][:, a, :].bitcast(F32)
                xt = psum.tile([P, PASSES * 2, P], F32)
                for gu in range(PASSES * 2):
                    nc.tensor.transpose(xt[:, gu, :], words[:, P * gu : P * (gu + 1)], ident[:])
                nc.scalar.copy(
                    out=grouped[:, a].bitcast(F32),
                    in_=xt[:].rearrange("p (g u) r -> p g r u", u=2),
                )
            return grouped

        def quantise_pair(grouped):
            x_codes = work.tile([P, PAIR, PASSES, P], U32, align_bytes=64)
            x_scales = work.tile([P, PAIR, PASSES, P], U8, align_bytes=64)
            nc.vector.quantize_mx(
                out=x_codes[:].rearrange("p a g r -> p (a g r)").bitcast(FP8X4),
                scales=x_scales[:].rearrange("p a g r -> p (a g r)"),
                in_=grouped[:].rearrange("p a g r t -> p (a g r t)"),
            )
            return x_codes, x_scales


        w_grouped = const.tile([P, PASSES, COLS, PACK], BF16, align_bytes=64)
        w_codes = const.tile([P, PASSES, COLS], U32, align_bytes=64)
        w_scales = const.tile([P, PASSES, COLS], U8, align_bytes=64)

        def regroup_views(g, s, part):
            c0, width = part
            cols = slice(BLOCK * s + c0, BLOCK * s + c0 + width)
            rows = w_rows[:, PACK * g : PACK * (g + 1), cols]
            return (
                w_grouped[:, g, cols, :].rearrange("p (c i) t -> p c t i", i=4),
                rows.rearrange("p t (c i) -> p c t i", i=4),
            )

        def regroup_w(g, s):
            wide_out, wide_in = regroup_views(g, s, PARTS[0])
            nc.vector.tensor_copy(out=wide_out, in_=wide_in)
            narrow_out, narrow_in = regroup_views(g, s, PARTS[1])
            nc.scalar.copy(out=narrow_out, in_=narrow_in)

        def quantise_w(g, s):
            for c0, width in PARTS:
                cols = slice(BLOCK * s + c0, BLOCK * s + c0 + width)
                nc.vector.quantize_mx(
                    out=w_codes[:, g, cols].bitcast(FP8X4),
                    scales=w_scales[:, g, cols],
                    in_=w_grouped[:, g, cols, :].rearrange("p c t -> p (c t)"),
                )

        pieces = [(g, s) for g in range(PASSES) for s in range(3)]
        for n, (g, s) in enumerate(pieces):
            regroup_w(g, s)
            if n > 0:
                quantise_w(*pieces[n - 1])
        quantise_w(*pieces[-1])
        ready = quantise_pair(transpose_pair(0))
        make_factors(0)

        def project(x_codes, x_scales, a):
            ps_q = psum.tile([P, BANK], F32)
            ps_k = psum.tile([P, BANK], F32)
            ps_v = psum.tile([P, BANK], F32)
            for s, bank in enumerate((ps_q, ps_k, ps_v)):
                for c0, width in PARTS:
                    cols = slice(BLOCK * s + c0, BLOCK * s + c0 + width)
                    for g in range(PASSES):
                        nc.tensor.matmul_mx(
                            out=bank[:, c0 : c0 + width],
                            lhsT=x_codes[:, a, g, :].bitcast(FP8X4),
                            lhsT_scale=x_scales[:, a, g, :],
                            rhs=w_codes[:, g, cols].bitcast(FP8X4),
                            rhs_scale=w_scales[:, g, cols],
                            start=(g == 0),
                            stop=(g == PASSES - 1),
                        )
            return ps_q, ps_k, ps_v

        def rope_and_collect(banks, t, staged, slot):
            ps_q, ps_k, ps_v = banks
            products = work.tile([P, 2, 2, BLOCK], F32)
            shape = [P, 2, HEADS, HEAD_DIM]
            for s, bank in enumerate((ps_q, ps_k)):
                by_head = bank[:, :BLOCK].rearrange("p (h d) -> p h d", h=HEADS)
                nc.vector.tensor_tensor(
                    out=products[:, :, s, :].rearrange("p c (h d) -> p c h d", h=HEADS),
                    in0=by_head.unsqueeze(1).to_broadcast(shape),
                    in1=factors[:, t].unsqueeze(2).to_broadcast(shape),
                    op=MULT,
                )
            split = "p s (h a f j) -> p (s h) a f j"
            own_part = products[:, 0].rearrange(split, h=HEADS, a=AXES, f=2)
            partner_part = products[:, 1].rearrange(split, h=HEADS, a=AXES, f=2)
            rotated = staged[:, 0:2, :, slot, :].rearrange(
                "p s h (a f j) -> p (s h) a f j", a=AXES, f=2
            )
            adder = nc.vector if t % VECTOR_ADDS_EVERY == VECTOR_ADDS_EVERY - 1 else nc.gpsimd
            for f in range(2):
                adder.tensor_tensor(
                    out=rotated[:, :, :, f, :],
                    in0=own_part[:, :, :, f, :],
                    in1=partner_part[:, :, :, 1 - f, :],
                    op=ADD,
                )
            nc.scalar.copy(
                out=staged[:, 2, :, slot, :],
                in_=ps_v[:, :BLOCK].rearrange("p (h d) -> p h d", h=HEADS),
            )

        def store(b, t0, count, staged, slot0):
            for s, out in enumerate(outs):
                by_partition = out[b].rearrange("h (p t) d -> p h t d", t=TILES)
                nc.sync.dma_start(
                    out=by_partition[:, :, t0 : t0 + count, :],
                    in_=staged[:, s, :, slot0 : slot0 + count, :],
                )

        staged = None
        for i in range(PAIRS):
            x_codes, x_scales = ready
            b, t0 = divmod(i * PAIR, TILES)
            slot0 = t0 % GROUP
            if slot0 == 0:
                staged = work.tile([P, 3, HEADS, GROUP, HEAD_DIM], F32)
                next_group = t0 // GROUP + 1
                if b == 0 and next_group < TILES // GROUP:
                    make_factors(next_group)
            grouped = transpose_pair(i + 1) if i + 1 < PAIRS else None
            rope_and_collect(project(x_codes, x_scales, 0), t0, staged, slot0)
            if grouped is not None:
                ready = quantise_pair(grouped)
            rope_and_collect(project(x_codes, x_scales, 1), t0 + 1, staged, slot0 + 1)
            if i * PAIR >= BATCH * TILES - GROUP:
                store(b, t0, PAIR, staged, slot0)
            elif slot0 + PAIR == GROUP:
                store(b, t0 + PAIR - GROUP, GROUP, staged, 0)
